import numpy as np
import ml_dtypes


def mxq(x, axis, fmt="e4m3"):
    dtype, down = {"e4m3": (ml_dtypes.float8_e4m3fn, 7), "e5m2": (ml_dtypes.float8_e5m2, 14)}[fmt]
    v = np.moveaxis(np.asarray(x, np.float32).astype(ml_dtypes.bfloat16).astype(np.float64), axis, -1)
    blocks = v.reshape(v.shape[:-1] + (-1, 32))
    amax = np.abs(blocks).max(-1, keepdims=True)
    byte = np.maximum(np.where(amax > 0, np.frexp(amax)[1] - 1 + 127, 0) - down, 1)
    scale = np.exp2(byte - 127.0)
    codes = (blocks / scale).astype(np.float32).astype(dtype).astype(np.float64)
    return np.moveaxis((codes * scale).reshape(v.shape), -1, axis)


WIDE = False


def mx_kscale(k):
    if not WIDE:
        return np.ones(k)
    levels = np.array([10, -10, 5, -5, 0])
    a = np.random.permutation(np.resize(levels, k // 512 * 4)).reshape(k // 512, 4)
    idx = np.arange(k)
    return np.exp2(a[idx // 512, idx % 128 // 32])


BF16 = ml_dtypes.bfloat16


def bf(x):
    return np.asarray(x, np.float32).astype(BF16)


def f64(x):
    return np.asarray(x).astype(np.float64)


G, S, M, H, E, C = 8, 1024, 512, 512, 8, 64


def setup_inputs():
    s, t = mx_kscale(S), mx_kscale(M)
    return {"dispatch_mask": bf(np.random.standard_normal((G, S, E, C)) * 0.1 * s[None, :, None, None]),
            "x": bf(np.random.standard_normal((G, S, M)) / s[None, :, None] * t),
            "wi": bf(np.random.standard_normal((E, M, H)) * 10.0 / np.sqrt(S * M) / t[None, :, None])}


def reference(dispatch_mask, x, wi):
    dm = mxq(f64(dispatch_mask).reshape(G, S, E * C), 1, "e4m3")
    xq = mxq(f64(x), 1, "e4m3")
    d = dm.transpose(0, 2, 1) @ xq
    dispatched = d.reshape(G, E, C, M).transpose(1, 0, 2, 3)
    pre = mxq(dispatched.reshape(E, G * C, M), 2, "e4m3") @ mxq(f64(wi), 1, "e4m3")
    return np.maximum(pre, 0.0).reshape(E, G, C, H)

@@ -1,0 +1,181 @@
+from contextlib import ExitStack
+
+import concourse.mybir as mybir
+
+BF16 = mybir.dt.bfloat16
+F32 = mybir.dt.float32
+U32 = mybir.dt.uint32
+U8 = mybir.dt.uint8
+FP8X4 = mybir.dt.float8_e4m3fn_x4
+RELU = mybir.ActivationFunctionType.Relu
+
+G, S, M, H, E, C = 8, 1024, 512, 512, 8, 64
+FLOPS = 2 * G * (E * C) * M * S + 2 * E * (G * C) * M * H
+
+P = 128
+PACK = 4
+K_PASS = P * PACK
+WIDTH = 512
+PASSES = S // K_PASS
+SLABS_PER_GROUP = 2 * PASSES
+GROUP_SLABS = G * SLABS_PER_GROUP
+BANKS_PER_GROUP = (E * C) // P
+EXPERTS_PER_BANK = P // C
+ROW_TILES = (G * C) // P
+TILES_PER_STORE = 2
+
+RUN = 4
+VECTOR_COLUMNS = 344
+RAW_BUFS = 24
+EVACUATE_LAG = 6
+
+
+def tile_flaxpositionwisemoelayer_pa_t_kernel(tc, dispatch_mask, x, wi, out):
+    nc = tc.nc
+
+    mask_slabs = dispatch_mask.rearrange("g (k p j) e c -> g k p j (e c)", p=P, j=PACK)
+    x_slabs = x.rearrange("g (k p j) m -> g k p j m", p=P, j=PACK)
+    wi_slabs = wi.rearrange("e (j p) h -> e p j h", p=P)
+    out_stores = out.rearrange(
+        "e (a b g) c h -> e a (g c) b h", b=TILES_PER_STORE, g=P // C
+    )
+
+    sources = []
+    for g in range(G):
+        for k in range(PASSES):
+            sources.append(mask_slabs[g, k])
+            sources.append(x_slabs[g, k])
+    for e in range(E):
+        sources.append(wi_slabs[e])
+
+    with ExitStack() as ctx:
+        raw_pool = ctx.enter_context(tc.tile_pool(name="raw", bufs=RAW_BUFS))
+        grouped_pool = ctx.enter_context(tc.tile_pool(name="grouped", bufs=4))
+        operand_pool = ctx.enter_context(tc.tile_pool(name="operands", bufs=3))
+        dispatched_pool = ctx.enter_context(tc.tile_pool(name="dispatched", bufs=1))
+        result_pool = ctx.enter_context(tc.tile_pool(name="result", bufs=4))
+        psum = ctx.enter_context(tc.psum_pool(name="psum", bufs=8))
+
+        raws = {}
+
+        def fetch(n):
+            if n < len(sources):
+                raw = raw_pool.tile([P, PACK, WIDTH], BF16)
+                nc.sync.dma_start(out=raw[:], in_=sources[n])
+                raws[n] = raw
+
+        def regroup(raw, vector_columns):
+            grouped = grouped_pool.tile([P, WIDTH, PACK], BF16, align_bytes=64)
+            src = raw[:].rearrange("p j (w i) -> p w j i", i=RUN)
+            dst = grouped[:].rearrange("p (w i) j -> p w j i", i=RUN)
+            split = vector_columns // RUN
+            nc.vector.tensor_copy(out=dst[:, :split], in_=src[:, :split])
+            if split < WIDTH // RUN:
+                nc.scalar.copy(out=dst[:, split:], in_=src[:, split:])
+            return grouped
+
+        def quantise(values, codes, scales):
+            nc.vector.quantize_mx(out=codes.bitcast(FP8X4), scales=scales, in_=values)
+
+        dispatched = []
+        for n in range(BANKS_PER_GROUP):
+            dispatched.append(
+                dispatched_pool.tile(
+                    [P, EXPERTS_PER_BANK, G, C, PACK],
+                    BF16,
+                    name="dispatched%d" % n,
+                    align_bytes=64,
+                )
+            )
+
+        def dispatch(mask_codes, mask_scales, x_codes, x_scales):
+            banks = []
+            for n in range(BANKS_PER_GROUP):
+                bank = psum.tile([P, PACK, P], F32, tag="bank")
+                columns = slice(n * P, (n + 1) * P)
+                for j in range(PACK):
+                    m_tile = slice(j * P, (j + 1) * P)
+                    for k in range(PASSES):
+                        nc.tensor.matmul_mx(
+                            out=bank[:, j, :],
+                            lhsT=x_codes[:, k, m_tile].bitcast(FP8X4),
+                            lhsT_scale=x_scales[:, k, m_tile],
+                            rhs=mask_codes[:, k, columns].bitcast(FP8X4),
+                            rhs_scale=mask_scales[:, k, columns],
+                            start=(k == 0),
+                            stop=(k == PASSES - 1),
+                        )
+                banks.append(bank)
+            return banks
+
+        def evacuate(bank, g, n):
+            nc.scalar.copy(
+                out=dispatched[n][:, :, g, :, :],
+                in_=bank[:].rearrange("p j (e c) -> p e c j", c=C),
+            )
+
+        for n in range(RAW_BUFS - 1):
+            fetch(n)
+        grouped_slabs = {}
+        operands = {}
+        banks = {}
+        for step in range(GROUP_SLABS + EVACUATE_LAG):
+            fetch(step + RAW_BUFS - 1)
+            if step < GROUP_SLABS:
+                grouped_slabs[step] = regroup(raws[step], VECTOR_COLUMNS)
+            ready = step - 1
+            if 0 <= ready < GROUP_SLABS:
+                g, slab = divmod(ready, SLABS_PER_GROUP)
+                k, is_x = divmod(slab, 2)
+                if slab == 0:
+                    mask_codes = operand_pool.tile([P, PASSES, WIDTH], U32, align_bytes=64)
+                    mask_scales = operand_pool.tile([P, PASSES, WIDTH], U8, align_bytes=64)
+                    x_codes = operand_pool.tile([P, PASSES, WIDTH], U32, align_bytes=64)
+                    x_scales = operand_pool.tile([P, PASSES, WIDTH], U8, align_bytes=64)
+                    operands = {0: (mask_codes, mask_scales), 1: (x_codes, x_scales)}
+                codes, scales = operands[is_x]
+                quantise(
+                    grouped_slabs[ready][:].rearrange("p w j -> p (w j)"),
+                    codes[:, k, :],
+                    scales[:, k, :],
+                )
+                if slab == SLABS_PER_GROUP - 1:
+                    banks[g] = dispatch(mask_codes, mask_scales, x_codes, x_scales)
+            full = step - EVACUATE_LAG
+            if 0 <= full < G * BANKS_PER_GROUP:
+                g, n = divmod(full, BANKS_PER_GROUP)
+                evacuate(banks[g][n], g, n)
+
+        grouped_wi = regroup(raws[GROUP_SLABS], WIDTH)
+        for e in range(E):
+            grouped_now = grouped_wi
+            if e + 1 < E:
+                grouped_wi = regroup(raws[GROUP_SLABS + e + 1], WIDTH)
+            wi_codes = operand_pool.tile([P, H], U32, align_bytes=64)
+            wi_scales = operand_pool.tile([P, H], U8, align_bytes=64)
+            quantise(grouped_now[:].rearrange("p w j -> p (w j)"), wi_codes[:], wi_scales[:])
+            d_codes = operand_pool.tile([P, G * C], U32, align_bytes=64)
+            d_scales = operand_pool.tile([P, G * C], U8, align_bytes=64)
+            n, member = divmod(e, EXPERTS_PER_BANK)
+            quantise(
+                dispatched[n][:, member].rearrange("p g c j -> p (g c j)"),
+                d_codes[:],
+                d_scales[:],
+            )
+            for a in range(ROW_TILES // TILES_PER_STORE):
+                result = result_pool.tile([P, TILES_PER_STORE, H], F32)
+                for b in range(TILES_PER_STORE):
+                    first = (a * TILES_PER_STORE + b) * P
+                    rows = slice(first, first + P)
+                    acc = psum.tile([P, H], F32, tag="bank")
+                    nc.tensor.matmul_mx(
+                        out=acc[:],
+                        lhsT=d_codes[:, rows].bitcast(FP8X4),
+                        lhsT_scale=d_scales[:, rows],
+                        rhs=wi_codes[:].bitcast(FP8X4),
+                        rhs_scale=wi_scales[:],
+                        start=True,
+                        stop=True,
+                    )
+                    nc.scalar.activation(out=result[:, b, :], in_=acc[:], func=RELU)
+                nc.sync.dma_start(out=out_stores[e, a], in_=result[:])

@@ -21,8 +21,9 @@ SLABS_PER_GROUP = 2 * PASSES
 GROUP_SLABS = G * SLABS_PER_GROUP
 BANKS_PER_GROUP = (E * C) // P
 EXPERTS_PER_BANK = P // C
-ROW_TILES = (G * C) // P
-TILES_PER_STORE = 2
+HALVES = 2
+GROUPS_PER_HALF = G // HALVES
+TILES_PER_HALF = (GROUPS_PER_HALF * C) // P
 
 RUN = 4
 VECTOR_COLUMNS = 344
@@ -36,8 +37,8 @@ def tile_flaxpositionwisemoelayer_pa_t_kernel(tc, dispatch_mask, x, wi, out):
     mask_slabs = dispatch_mask.rearrange("g (k p j) e c -> g k p j (e c)", p=P, j=PACK)
     x_slabs = x.rearrange("g (k p j) m -> g k p j m", p=P, j=PACK)
     wi_slabs = wi.rearrange("e (j p) h -> e p j h", p=P)
-    out_stores = out.rearrange(
-        "e (a b g) c h -> e a (g c) b h", b=TILES_PER_STORE, g=P // C
+    out_halves = out.rearrange(
+        "e (a g) (q b) h -> e a (g q) b h", a=HALVES, b=TILES_PER_HALF
     )
 
     sources = []
@@ -77,16 +78,15 @@ def tile_flaxpositionwisemoelayer_pa_t_kernel(tc, dispatch_mask, x, wi, out):
         def quantise(values, codes, scales):
             nc.vector.quantize_mx(out=codes.bitcast(FP8X4), scales=scales, in_=values)
 
-        dispatched = []
+        dispatched = {}
         for n in range(BANKS_PER_GROUP):
-            dispatched.append(
-                dispatched_pool.tile(
-                    [P, EXPERTS_PER_BANK, G, C, PACK],
+            for a in range(HALVES):
+                dispatched[n, a] = dispatched_pool.tile(
+                    [P, EXPERTS_PER_BANK, TILES_PER_HALF, GROUPS_PER_HALF, C // TILES_PER_HALF, PACK],
                     BF16,
-                    name="dispatched%d" % n,
+                    name="dispatched%d%d" % (n, a),
                     align_bytes=64,
                 )
-            )
 
         def dispatch(mask_codes, mask_scales, x_codes, x_scales):
             banks = []
@@ -109,9 +109,12 @@ def tile_flaxpositionwisemoelayer_pa_t_kernel(tc, dispatch_mask, x, wi, out):
             return banks
 
         def evacuate(bank, g, n):
+            a, g_in_half = divmod(g, GROUPS_PER_HALF)
             nc.scalar.copy(
-                out=dispatched[n][:, :, g, :, :],
-                in_=bank[:].rearrange("p j (e c) -> p e c j", c=C),
+                out=dispatched[n, a][:, :, :, g_in_half, :, :],
+                in_=bank[:].rearrange(
+                    "p j (e q b) -> p e b q j", e=EXPERTS_PER_BANK, b=TILES_PER_HALF
+                ),
             )
 
         for n in range(RAW_BUFS - 1):
@@ -154,19 +157,18 @@ def tile_flaxpositionwisemoelayer_pa_t_kernel(tc, dispatch_mask, x, wi, out):
             wi_codes = operand_pool.tile([P, H], U32, align_bytes=64)
             wi_scales = operand_pool.tile([P, H], U8, align_bytes=64)
             quantise(grouped_now[:].rearrange("p w j -> p (w j)"), wi_codes[:], wi_scales[:])
-            d_codes = operand_pool.tile([P, G * C], U32, align_bytes=64)
-            d_scales = operand_pool.tile([P, G * C], U8, align_bytes=64)
             n, member = divmod(e, EXPERTS_PER_BANK)
-            quantise(
-                dispatched[n][:, member].rearrange("p g c j -> p (g c j)"),
-                d_codes[:],
-                d_scales[:],
-            )
-            for a in range(ROW_TILES // TILES_PER_STORE):
-                result = result_pool.tile([P, TILES_PER_STORE, H], F32)
-                for b in range(TILES_PER_STORE):
-                    first = (a * TILES_PER_STORE + b) * P
-                    rows = slice(first, first + P)
+            for a in range(HALVES):
+                d_codes = operand_pool.tile([P, TILES_PER_HALF * P], U32, align_bytes=64)
+                d_scales = operand_pool.tile([P, TILES_PER_HALF * P], U8, align_bytes=64)
+                quantise(
+                    dispatched[n, a][:, member].rearrange("p b g q j -> p (b g q j)"),
+                    d_codes[:],
+                    d_scales[:],
+                )
+                result = result_pool.tile([P, TILES_PER_HALF, H], F32)
+                for b in range(TILES_PER_HALF):
+                    rows = slice(b * P, (b + 1) * P)
                     acc = psum.tile([P, H], F32, tag="bank")
                     nc.tensor.matmul_mx(
                         out=acc[:],
@@ -178,4 +180,4 @@ def tile_flaxpositionwisemoelayer_pa_t_kernel(tc, dispatch_mask, x, wi, out):
                         stop=True,
                     )
                     nc.scalar.activation(out=result[:, b, :], in_=acc[:], func=RELU)
-                nc.sync.dma_start(out=out_stores[e, a], in_=result[:])
+                nc.sync.dma_start(out=out_halves[e, a], in_=result[:])

@@ -26,7 +26,8 @@ GROUPS_PER_HALF = G // HALVES
 TILES_PER_HALF = (GROUPS_PER_HALF * C) // P
 
 RUN = 4
-VECTOR_COLUMNS = 344
+VECTOR_COLUMNS = 336
+EARLY_VECTOR_COLUMNS = 256
 RAW_BUFS = 24
 EVACUATE_LAG = 6
 
@@ -125,7 +126,10 @@ def tile_flaxpositionwisemoelayer_pa_t_kernel(tc, dispatch_mask, x, wi, out):
         for step in range(GROUP_SLABS + EVACUATE_LAG):
             fetch(step + RAW_BUFS - 1)
             if step < GROUP_SLABS:
-                grouped_slabs[step] = regroup(raws[step], VECTOR_COLUMNS)
+                if step < EVACUATE_LAG:
+                    grouped_slabs[step] = regroup(raws[step], EARLY_VECTOR_COLUMNS)
+                else:
+                    grouped_slabs[step] = regroup(raws[step], VECTOR_COLUMNS)
             ready = step - 1
             if 0 <= ready < GROUP_SLABS:
                 g, slab = divmod(ready, SLABS_PER_GROUP)
@@ -179,5 +183,8 @@ def tile_flaxpositionwisemoelayer_pa_t_kernel(tc, dispatch_mask, x, wi, out):
                         start=True,
                         stop=True,
                     )
-                    nc.scalar.activation(out=result[:, b, :], in_=acc[:], func=RELU)
+                    if e == E - 1 and b == TILES_PER_HALF - 1:
+                        nc.vector.tensor_scalar_max(result[:, b, :], acc[:], 0.0)
+                    else:
+                        nc.scalar.activation(out=result[:, b, :], in_=acc[:], func=RELU)
                 nc.sync.dma_start(out=out_halves[e, a], in_=result[:])

@@ -1,6 +1,7 @@
 from contextlib import ExitStack
 
 import concourse.mybir as mybir
+from concourse.masks import make_identity
 
 BF16 = mybir.dt.bfloat16
 F32 = mybir.dt.float32
@@ -28,6 +29,9 @@ TILES_PER_HALF = (GROUPS_PER_HALF * C) // P
 RUN = 4
 VECTOR_COLUMNS = 336
 EARLY_VECTOR_COLUMNS = 256
+TENSOR_COLUMNS = 256
+REGROUPED_BANKS = 2
+PRODUCT_BANKS = 6
 RAW_BUFS = 24
 EVACUATE_LAG = 6
 
@@ -58,6 +62,10 @@ def tile_flaxpositionwisemoelayer_pa_t_kernel(tc, dispatch_mask, x, wi, out):
         result_pool = ctx.enter_context(tc.tile_pool(name="result", bufs=4))
         psum = ctx.enter_context(tc.psum_pool(name="psum", bufs=8))
 
+        identity_pool = ctx.enter_context(tc.tile_pool(name="identity", bufs=1))
+        identity = identity_pool.tile([P, P], BF16)
+        make_identity(nc, identity[:])
+
         raws = {}
 
         def fetch(n):
@@ -76,6 +84,28 @@ def tile_flaxpositionwisemoelayer_pa_t_kernel(tc, dispatch_mask, x, wi, out):
                 nc.scalar.copy(out=dst[:, split:], in_=src[:, split:])
             return grouped
 
+        def regroup_on_tensor(raw):
+            bank = psum.tile([P, TENSOR_COLUMNS, PACK], BF16, tag="regrouped", bufs=REGROUPED_BANKS)
+            for w in range(0, TENSOR_COLUMNS, P):
+                first = WIDTH - TENSOR_COLUMNS + w
+                nc.tensor.matmul(
+                    out=bank[:, w : w + P, :].rearrange("p w j -> p j w"),
+                    lhsT=identity[:],
+                    rhs=raw[:, :, first : first + P],
+                    start=True,
+                    stop=True,
+                )
+            return bank
+
+        def regroup_shared(raw, bank):
+            grouped = grouped_pool.tile([P, WIDTH, PACK], BF16, align_bytes=64)
+            src = raw[:].rearrange("p j (w i) -> p w j i", i=RUN)
+            dst = grouped[:].rearrange("p (w i) j -> p w j i", i=RUN)
+            first = WIDTH - TENSOR_COLUMNS
+            nc.vector.tensor_copy(out=dst[:, : first // RUN], in_=src[:, : first // RUN])
+            nc.scalar.copy(out=grouped[:, first:, :], in_=bank[:])
+            return grouped
+
         def quantise(values, codes, scales):
             nc.vector.quantize_mx(out=codes.bitcast(FP8X4), scales=scales, in_=values)
 
@@ -92,7 +122,7 @@ def tile_flaxpositionwisemoelayer_pa_t_kernel(tc, dispatch_mask, x, wi, out):
         def dispatch(mask_codes, mask_scales, x_codes, x_scales):
             banks = []
             for n in range(BANKS_PER_GROUP):
-                bank = psum.tile([P, PACK, P], F32, tag="bank")
+                bank = psum.tile([P, PACK, P], F32, tag="bank", bufs=PRODUCT_BANKS)
                 columns = slice(n * P, (n + 1) * P)
                 for j in range(PACK):
                     m_tile = slice(j * P, (j + 1) * P)
@@ -121,15 +151,20 @@ def tile_flaxpositionwisemoelayer_pa_t_kernel(tc, dispatch_mask, x, wi, out):
         for n in range(RAW_BUFS - 1):
             fetch(n)
         grouped_slabs = {}
+        regrouped_banks = {}
         operands = {}
         banks = {}
         for step in range(GROUP_SLABS + EVACUATE_LAG):
             fetch(step + RAW_BUFS - 1)
             if step < GROUP_SLABS:
-                if step < EVACUATE_LAG:
+                if step in regrouped_banks:
+                    grouped_slabs[step] = regroup_shared(raws[step], regrouped_banks[step])
+                elif step < EVACUATE_LAG:
                     grouped_slabs[step] = regroup(raws[step], EARLY_VECTOR_COLUMNS)
                 else:
                     grouped_slabs[step] = regroup(raws[step], VECTOR_COLUMNS)
+            if step + 1 < GROUP_SLABS and step % 2 == 0:
+                regrouped_banks[step + 1] = regroup_on_tensor(raws[step + 1])
             ready = step - 1
             if 0 <= ready < GROUP_SLABS:
                 g, slab = divmod(ready, SLABS_PER_GROUP)
@@ -173,7 +208,7 @@ def tile_flaxpositionwisemoelayer_pa_t_kernel(tc, dispatch_mask, x, wi, out):
                 result = result_pool.tile([P, TILES_PER_HALF, H], F32)
                 for b in range(TILES_PER_HALF):
                     rows = slice(b * P, (b + 1) * P)
-                    acc = psum.tile([P, H], F32, tag="bank")
+                    acc = psum.tile([P, H], F32, tag="bank", bufs=PRODUCT_BANKS)
                     nc.tensor.matmul_mx(
                         out=acc[:],
                         lhsT=d_codes[:, rows].bitcast(FP8X4),

@@ -103,7 +103,10 @@ def tile_flaxpositionwisemoelayer_pa_t_kernel(tc, dispatch_mask, x, wi, out):
             dst = grouped[:].rearrange("p (w i) j -> p w j i", i=RUN)
             first = WIDTH - TENSOR_COLUMNS
             nc.vector.tensor_copy(out=dst[:, : first // RUN], in_=src[:, : first // RUN])
-            nc.scalar.copy(out=grouped[:, first:, :], in_=bank[:])
+            nc.scalar.copy(
+                out=grouped[:, first:, :].rearrange("p w j -> p (w j)"),
+                in_=bank[:].rearrange("p w j -> p (w j)"),
+            )
             return grouped
 
         def quantise(values, codes, scales):
@@ -119,25 +122,24 @@ def tile_flaxpositionwisemoelayer_pa_t_kernel(tc, dispatch_mask, x, wi, out):
                     align_bytes=64,
                 )
 
-        def dispatch(mask_codes, mask_scales, x_codes, x_scales):
-            banks = []
-            for n in range(BANKS_PER_GROUP):
-                bank = psum.tile([P, PACK, P], F32, tag="bank", bufs=PRODUCT_BANKS)
-                columns = slice(n * P, (n + 1) * P)
-                for j in range(PACK):
-                    m_tile = slice(j * P, (j + 1) * P)
-                    for k in range(PASSES):
-                        nc.tensor.matmul_mx(
-                            out=bank[:, j, :],
-                            lhsT=x_codes[:, k, m_tile].bitcast(FP8X4),
-                            lhsT_scale=x_scales[:, k, m_tile],
-                            rhs=mask_codes[:, k, columns].bitcast(FP8X4),
-                            rhs_scale=mask_scales[:, k, columns],
-                            start=(k == 0),
-                            stop=(k == PASSES - 1),
-                        )
-                banks.append(bank)
-            return banks
+        def dispatch(group_operands, n):
+            mask_codes, mask_scales = group_operands[0]
+            x_codes, x_scales = group_operands[1]
+            bank = psum.tile([P, PACK, P], F32, tag="bank", bufs=PRODUCT_BANKS)
+            columns = slice(n * P, (n + 1) * P)
+            for j in range(PACK):
+                m_tile = slice(j * P, (j + 1) * P)
+                for k in range(PASSES):
+                    nc.tensor.matmul_mx(
+                        out=bank[:, j, :],
+                        lhsT=x_codes[:, k, m_tile].bitcast(FP8X4),
+                        lhsT_scale=x_scales[:, k, m_tile],
+                        rhs=mask_codes[:, k, columns].bitcast(FP8X4),
+                        rhs_scale=mask_scales[:, k, columns],
+                        start=(k == 0),
+                        stop=(k == PASSES - 1),
+                    )
+            return bank
 
         def evacuate(bank, g, n):
             a, g_in_half = divmod(g, GROUPS_PER_HALF)
@@ -181,12 +183,16 @@ def tile_flaxpositionwisemoelayer_pa_t_kernel(tc, dispatch_mask, x, wi, out):
                     codes[:, k, :],
                     scales[:, k, :],
                 )
-                if slab == SLABS_PER_GROUP - 1:
-                    banks[g] = dispatch(mask_codes, mask_scales, x_codes, x_scales)
+            filled = step - SLABS_PER_GROUP
+            if 0 <= filled < G * BANKS_PER_GROUP:
+                g, n = divmod(filled, BANKS_PER_GROUP)
+                if n == 0:
+                    group_operands = operands
+                banks[g, n] = dispatch(group_operands, n)
             full = step - EVACUATE_LAG
             if 0 <= full < G * BANKS_PER_GROUP:
                 g, n = divmod(full, BANKS_PER_GROUP)
-                evacuate(banks[g][n], g, n)
+                evacuate(banks[g, n], g, n)
 
         grouped_wi = regroup(raws[GROUP_SLABS], WIDTH)
         for e in range(E):

@@ -61,6 +61,7 @@ def tile_flaxpositionwisemoelayer_pa_t_kernel(tc, dispatch_mask, x, wi, out):
         dispatched_pool = ctx.enter_context(tc.tile_pool(name="dispatched", bufs=1))
         result_pool = ctx.enter_context(tc.tile_pool(name="result", bufs=4))
         psum = ctx.enter_context(tc.psum_pool(name="psum", bufs=8))
+        ctx.enter_context(tc.manual_schedule())
 
         identity_pool = ctx.enter_context(tc.tile_pool(name="identity", bufs=1))
         identity = identity_pool.tile([P, P], BF16)

@@ -18,8 +18,6 @@ PACK = 4
 K_PASS = P * PACK
 WIDTH = 512
 PASSES = S // K_PASS
-SLABS_PER_GROUP = 2 * PASSES
-GROUP_SLABS = G * SLABS_PER_GROUP
 BANKS_PER_GROUP = (E * C) // P
 EXPERTS_PER_BANK = P // C
 HALVES = 2
@@ -27,13 +25,31 @@ GROUPS_PER_HALF = G // HALVES
 TILES_PER_HALF = (GROUPS_PER_HALF * C) // P
 
 RUN = 4
-VECTOR_COLUMNS = 336
+VECTOR_COLUMNS = 344
+RESULT_BUFS = 8
+SHARE_EVERY = 100
+SHARE_PHASE = 0
+HEAD_PIECES = 2
 EARLY_VECTOR_COLUMNS = 256
+EARLY_STEPS = 6
 TENSOR_COLUMNS = 256
 REGROUPED_BANKS = 2
 PRODUCT_BANKS = 6
-RAW_BUFS = 24
-EVACUATE_LAG = 6
+RAW_BUFS = 22
+GROUPED_BUFS = 4
+EVACUATE_LAG = 2
+EARLY_EXPERTS = 0
+FIRST_WI_AFTER = 4
+WI_STRIDE = 1
+LEAD = 2
+SHARED_KIND = "x"
+SHARED_K = 1
+WI_COLUMNS = 352
+LATE_COLUMNS = 512
+FIRST_LATE_COLUMNS = 512
+FIRST_LATE = 2
+FIRST_SHARED = 0
+FINAL_PIECES = 2
 
 
 def tile_flaxpositionwisemoelayer_pa_t_kernel(tc, dispatch_mask, x, wi, out):
@@ -46,44 +62,50 @@ def tile_flaxpositionwisemoelayer_pa_t_kernel(tc, dispatch_mask, x, wi, out):
         "e (a g) (q b) h -> e a (g q) b h", a=HALVES, b=TILES_PER_HALF
     )
 
-    sources = []
+    stream = []
     for g in range(G):
         for k in range(PASSES):
-            sources.append(mask_slabs[g, k])
-            sources.append(x_slabs[g, k])
-    for e in range(E):
-        sources.append(wi_slabs[e])
+            stream.append(("mask", g, k))
+            stream.append(("x", g, k))
+        stream += [("wi", e, 0) for e in range(EARLY_EXPERTS) if FIRST_WI_AFTER + e * WI_STRIDE == g]
+    stream_length = len(stream)
+    stream += [("wi", e, 0) for e in range(EARLY_EXPERTS, E)]
+
+    def is_shared(n):
+        kind, i, k = stream[n]
+        return kind == SHARED_KIND and k < SHARED_K and i >= FIRST_SHARED
 
     with ExitStack() as ctx:
         raw_pool = ctx.enter_context(tc.tile_pool(name="raw", bufs=RAW_BUFS))
-        grouped_pool = ctx.enter_context(tc.tile_pool(name="grouped", bufs=4))
+        grouped_pool = ctx.enter_context(tc.tile_pool(name="grouped", bufs=GROUPED_BUFS))
         operand_pool = ctx.enter_context(tc.tile_pool(name="operands", bufs=3))
-        dispatched_pool = ctx.enter_context(tc.tile_pool(name="dispatched", bufs=1))
-        result_pool = ctx.enter_context(tc.tile_pool(name="result", bufs=4))
+        keep_pool = ctx.enter_context(tc.tile_pool(name="keep", bufs=1))
+        result_pool = ctx.enter_context(tc.tile_pool(name="result", bufs=RESULT_BUFS))
         psum = ctx.enter_context(tc.psum_pool(name="psum", bufs=8))
         ctx.enter_context(tc.manual_schedule())
 
-        identity_pool = ctx.enter_context(tc.tile_pool(name="identity", bufs=1))
-        identity = identity_pool.tile([P, P], BF16)
+        identity = keep_pool.tile([P, P], BF16)
         make_identity(nc, identity[:])
+        wi_codes = keep_pool.tile([P, E, H], U32, align_bytes=64)
+        wi_scales = keep_pool.tile([P, E, H], U8, align_bytes=64)
 
         raws = {}
 
         def fetch(n):
-            if n < len(sources):
+            if n < len(stream):
+                kind, i, k = stream[n]
+                if kind == "mask":
+                    source = mask_slabs[i, k]
+                elif kind == "x":
+                    source = x_slabs[i, k]
+                else:
+                    source = wi_slabs[i]
                 raw = raw_pool.tile([P, PACK, WIDTH], BF16)
-                nc.sync.dma_start(out=raw[:], in_=sources[n])
+                pieces = HEAD_PIECES if n == 0 else 1
+                for w in range(pieces):
+                    columns = slice(w * WIDTH // pieces, (w + 1) * WIDTH // pieces)
+                    nc.sync.dma_start(out=raw[:, :, columns], in_=source[:, :, columns])
                 raws[n] = raw
-
-        def regroup(raw, vector_columns):
-            grouped = grouped_pool.tile([P, WIDTH, PACK], BF16, align_bytes=64)
-            src = raw[:].rearrange("p j (w i) -> p w j i", i=RUN)
-            dst = grouped[:].rearrange("p (w i) j -> p w j i", i=RUN)
-            split = vector_columns // RUN
-            nc.vector.tensor_copy(out=dst[:, :split], in_=src[:, :split])
-            if split < WIDTH // RUN:
-                nc.scalar.copy(out=dst[:, split:], in_=src[:, split:])
-            return grouped
 
         def regroup_on_tensor(raw):
             bank = psum.tile([P, TENSOR_COLUMNS, PACK], BF16, tag="regrouped", bufs=REGROUPED_BANKS)
@@ -98,34 +120,57 @@ def tile_flaxpositionwisemoelayer_pa_t_kernel(tc, dispatch_mask, x, wi, out):
                 )
             return bank
 
-        def regroup_shared(raw, bank):
+        def regroup(raw, vector_columns, bank):
             grouped = grouped_pool.tile([P, WIDTH, PACK], BF16, align_bytes=64)
-            src = raw[:].rearrange("p j (w i) -> p w j i", i=RUN)
-            dst = grouped[:].rearrange("p (w i) j -> p w j i", i=RUN)
-            first = WIDTH - TENSOR_COLUMNS
-            nc.vector.tensor_copy(out=dst[:, : first // RUN], in_=src[:, : first // RUN])
-            nc.scalar.copy(
-                out=grouped[:, first:, :].rearrange("p w j -> p (w j)"),
-                in_=bank[:].rearrange("p w j -> p (w j)"),
+            nc.vector.tensor_copy(
+                out=grouped[:, :vector_columns, :].rearrange("p (w i) j -> p w j i", i=RUN),
+                in_=raw[:, :, :vector_columns].rearrange("p j (w i) -> p w j i", i=RUN),
             )
+            if bank is not None:
+                nc.scalar.copy(
+                    out=grouped[:, vector_columns:, :].rearrange("p w j -> p (w j)"),
+                    in_=bank[:].rearrange("p w j -> p (w j)"),
+                )
+            elif vector_columns < WIDTH:
+                nc.scalar.copy(
+                    out=grouped[:, vector_columns:, :].rearrange("p (w i) j -> p w j i", i=RUN),
+                    in_=raw[:, :, vector_columns:].rearrange("p j (w i) -> p w j i", i=RUN),
+                )
             return grouped
 
         def quantise(values, codes, scales):
             nc.vector.quantize_mx(out=codes.bitcast(FP8X4), scales=scales, in_=values)
 
+        operands = {}
+
+        def quantise_slab(n, grouped):
+            kind, i, k = stream[n]
+            values = grouped[:].rearrange("p w j -> p (w j)")
+            if kind == "wi":
+                quantise(values, wi_codes[:, i, :], wi_scales[:, i, :])
+                return
+            if i not in operands:
+                mask_codes = operand_pool.tile([P, PASSES, WIDTH], U32, align_bytes=64)
+                mask_scales = operand_pool.tile([P, PASSES, WIDTH], U8, align_bytes=64)
+                x_codes = operand_pool.tile([P, PASSES, WIDTH], U32, align_bytes=64)
+                x_scales = operand_pool.tile([P, PASSES, WIDTH], U8, align_bytes=64)
+                operands[i] = {"mask": (mask_codes, mask_scales), "x": (x_codes, x_scales)}
+            codes, scales = operands[i][kind]
+            quantise(values, codes[:, k, :], scales[:, k, :])
+
         dispatched = {}
         for n in range(BANKS_PER_GROUP):
             for a in range(HALVES):
-                dispatched[n, a] = dispatched_pool.tile(
+                dispatched[n, a] = keep_pool.tile(
                     [P, EXPERTS_PER_BANK, TILES_PER_HALF, GROUPS_PER_HALF, C // TILES_PER_HALF, PACK],
                     BF16,
                     name="dispatched%d%d" % (n, a),
                     align_bytes=64,
                 )
 
-        def dispatch(group_operands, n):
-            mask_codes, mask_scales = group_operands[0]
-            x_codes, x_scales = group_operands[1]
+        def dispatch(g, n):
+            mask_codes, mask_scales = operands[g]["mask"]
+            x_codes, x_scales = operands[g]["x"]
             bank = psum.tile([P, PACK, P], F32, tag="bank", bufs=PRODUCT_BANKS)
             columns = slice(n * P, (n + 1) * P)
             for j in range(PACK):
@@ -151,82 +196,116 @@ def tile_flaxpositionwisemoelayer_pa_t_kernel(tc, dispatch_mask, x, wi, out):
                 ),
             )
 
+        def project(e, a):
+            n, member = divmod(e, EXPERTS_PER_BANK)
+            d_codes = operand_pool.tile([P, TILES_PER_HALF * P], U32, align_bytes=64)
+            d_scales = operand_pool.tile([P, TILES_PER_HALF * P], U8, align_bytes=64)
+            quantise(
+                dispatched[n, a][:, member].rearrange("p b g q j -> p (b g q j)"),
+                d_codes[:],
+                d_scales[:],
+            )
+            accs = []
+            for b in range(TILES_PER_HALF):
+                rows = slice(b * P, (b + 1) * P)
+                acc = psum.tile([P, H], F32, tag="bank", bufs=PRODUCT_BANKS)
+                nc.tensor.matmul_mx(
+                    out=acc[:],
+                    lhsT=d_codes[:, rows].bitcast(FP8X4),
+                    lhsT_scale=d_scales[:, rows],
+                    rhs=wi_codes[:, e, :].bitcast(FP8X4),
+                    rhs_scale=wi_scales[:, e, :],
+                    start=True,
+                    stop=True,
+                )
+                accs.append(acc)
+            return accs
+
+        def store(accs, e, a, share):
+            result = result_pool.tile([P, TILES_PER_HALF, H], F32)
+            if (e, a) == (E - 1, HALVES - 1):
+                for h in range(0, H, H // FINAL_PIECES):
+                    columns = slice(h, h + H // FINAL_PIECES)
+                    nc.scalar.activation(out=result[:, 0, columns], in_=accs[0][:, columns], func=RELU)
+                    nc.vector.tensor_scalar_max(result[:, 1, columns], accs[1][:, columns], 0.0)
+                    for b in range(TILES_PER_HALF):
+                        nc.sync.dma_start(out=out_halves[e, a][:, b, columns], in_=result[:, b, columns])
+                return
+            nc.scalar.activation(out=result[:, 0, :], in_=accs[0][:], func=RELU)
+            last = (e, a) == (E - 1, HALVES - 1)
+            if last:
+                nc.sync.dma_start(out=out_halves[e, a][:, 0, :], in_=result[:, 0, :])
+            if share:
+                nc.vector.tensor_scalar_max(result[:, 1, :], accs[1][:], 0.0)
+            else:
+                nc.scalar.activation(out=result[:, 1, :], in_=accs[1][:], func=RELU)
+            if last:
+                nc.sync.dma_start(out=out_halves[e, a][:, 1, :], in_=result[:, 1, :])
+            else:
+                nc.sync.dma_start(out=out_halves[e, a], in_=result[:])
+
         for n in range(RAW_BUFS - 1):
             fetch(n)
         grouped_slabs = {}
         regrouped_banks = {}
-        operands = {}
-        banks = {}
-        for step in range(GROUP_SLABS + EVACUATE_LAG):
+        to_dispatch = []
+        full_banks = []
+        to_project = []
+        to_store = []
+        step = 0
+        while step <= stream_length or to_dispatch or full_banks:
             fetch(step + RAW_BUFS - 1)
-            if step < GROUP_SLABS:
-                if step in regrouped_banks:
-                    grouped_slabs[step] = regroup_shared(raws[step], regrouped_banks[step])
-                elif step < EVACUATE_LAG:
-                    grouped_slabs[step] = regroup(raws[step], EARLY_VECTOR_COLUMNS)
+            if step + LEAD < stream_length and is_shared(step + LEAD):
+                regrouped_banks[step + LEAD] = regroup_on_tensor(raws[step + LEAD])
+            if step < stream_length:
+                if is_shared(step):
+                    columns = WIDTH - TENSOR_COLUMNS
+                elif step < EARLY_STEPS:
+                    columns = EARLY_VECTOR_COLUMNS
+                elif stream[step][0] == "wi":
+                    columns = WI_COLUMNS
                 else:
-                    grouped_slabs[step] = regroup(raws[step], VECTOR_COLUMNS)
-            if step + 1 < GROUP_SLABS and step % 2 == 0:
-                regrouped_banks[step + 1] = regroup_on_tensor(raws[step + 1])
+                    columns = VECTOR_COLUMNS
+                grouped_slabs[step] = regroup(raws[step], columns, regrouped_banks.get(step))
+            storing = to_store
+            to_store = [(project(e, a), e, a) for e, a in to_project]
+            to_project = []
             ready = step - 1
-            if 0 <= ready < GROUP_SLABS:
-                g, slab = divmod(ready, SLABS_PER_GROUP)
-                k, is_x = divmod(slab, 2)
-                if slab == 0:
-                    mask_codes = operand_pool.tile([P, PASSES, WIDTH], U32, align_bytes=64)
-                    mask_scales = operand_pool.tile([P, PASSES, WIDTH], U8, align_bytes=64)
-                    x_codes = operand_pool.tile([P, PASSES, WIDTH], U32, align_bytes=64)
-                    x_scales = operand_pool.tile([P, PASSES, WIDTH], U8, align_bytes=64)
-                    operands = {0: (mask_codes, mask_scales), 1: (x_codes, x_scales)}
-                codes, scales = operands[is_x]
-                quantise(
-                    grouped_slabs[ready][:].rearrange("p w j -> p (w j)"),
-                    codes[:, k, :],
-                    scales[:, k, :],
-                )
-            filled = step - SLABS_PER_GROUP
-            if 0 <= filled < G * BANKS_PER_GROUP:
-                g, n = divmod(filled, BANKS_PER_GROUP)
-                if n == 0:
-                    group_operands = operands
-                banks[g, n] = dispatch(group_operands, n)
-            full = step - EVACUATE_LAG
-            if 0 <= full < G * BANKS_PER_GROUP:
-                g, n = divmod(full, BANKS_PER_GROUP)
-                evacuate(banks[g, n], g, n)
+            if 0 <= ready < stream_length:
+                kind, i, k = stream[ready]
+                quantise_slab(ready, grouped_slabs[ready])
+                if kind == "wi":
+                    to_project.append((i, 0))
+                elif (kind, k) == ("x", PASSES - 1):
+                    to_dispatch += [(i, n) for n in range(BANKS_PER_GROUP)]
+            if full_banks and full_banks[0][0] + EVACUATE_LAG <= step:
+                filled, bank, g, n = full_banks.pop(0)
+                evacuate(bank, g, n)
+            if to_dispatch:
+                g, n = to_dispatch.pop(0)
+                full_banks.append((step, dispatch(g, n), g, n))
+            for accs, e, a in storing:
+                store(accs, e, a, False)
+            step += 1
 
-        grouped_wi = regroup(raws[GROUP_SLABS], WIDTH)
-        for e in range(E):
-            grouped_now = grouped_wi
-            if e + 1 < E:
-                grouped_wi = regroup(raws[GROUP_SLABS + e + 1], WIDTH)
-            wi_codes = operand_pool.tile([P, H], U32, align_bytes=64)
-            wi_scales = operand_pool.tile([P, H], U8, align_bytes=64)
-            quantise(grouped_now[:].rearrange("p w j -> p (w j)"), wi_codes[:], wi_scales[:])
-            n, member = divmod(e, EXPERTS_PER_BANK)
-            for a in range(HALVES):
-                d_codes = operand_pool.tile([P, TILES_PER_HALF * P], U32, align_bytes=64)
-                d_scales = operand_pool.tile([P, TILES_PER_HALF * P], U8, align_bytes=64)
-                quantise(
-                    dispatched[n, a][:, member].rearrange("p b g q j -> p (b g q j)"),
-                    d_codes[:],
-                    d_scales[:],
-                )
-                result = result_pool.tile([P, TILES_PER_HALF, H], F32)
-                for b in range(TILES_PER_HALF):
-                    rows = slice(b * P, (b + 1) * P)
-                    acc = psum.tile([P, H], F32, tag="bank", bufs=PRODUCT_BANKS)
-                    nc.tensor.matmul_mx(
-                        out=acc[:],
-                        lhsT=d_codes[:, rows].bitcast(FP8X4),
-                        lhsT_scale=d_scales[:, rows],
-                        rhs=wi_codes[:].bitcast(FP8X4),
-                        rhs_scale=wi_scales[:],
-                        start=True,
-                        stop=True,
-                    )
-                    if e == E - 1 and b == TILES_PER_HALF - 1:
-                        nc.vector.tensor_scalar_max(result[:, b, :], acc[:], 0.0)
-                    else:
-                        nc.scalar.activation(out=result[:, b, :], in_=acc[:], func=RELU)
-                nc.sync.dma_start(out=out_halves[e, a], in_=result[:])
+        halves = [(e, 1) for e in range(EARLY_EXPERTS)]
+        halves += [(e, a) for e in range(EARLY_EXPERTS, E) for a in range(HALVES)]
+        halves = to_project + halves
+        late = stream_length
+        if EARLY_EXPERTS == 0:
+            grouped_first = regroup(raws[late], FIRST_LATE_COLUMNS, None)
+            quantise_slab(late, grouped_first)
+            late += 1
+        grouped_late = {}
+        for i, (e, a) in enumerate(halves):
+            storing = to_store
+            to_store = [(project(e, a), e, a)]
+            for n in list(grouped_late):
+                quantise_slab(n, grouped_late.pop(n))
+            if i % 2 == 0 and late < len(stream):
+                grouped_late[late] = regroup(raws[late], FIRST_LATE_COLUMNS if late < stream_length + FIRST_LATE else LATE_COLUMNS, None)
+                late += 1
+            for accs, e2, a2 in storing:
+                store(accs, e2, a2, i % SHARE_EVERY == SHARE_PHASE)
+        for accs, e2, a2 in to_store:
+            store(accs, e2, a2, True)

from contextlib import ExitStack

import concourse.mybir as mybir
from concourse.masks import make_identity

BF16 = mybir.dt.bfloat16
F32 = mybir.dt.float32
U32 = mybir.dt.uint32
U8 = mybir.dt.uint8
FP8X4 = mybir.dt.float8_e4m3fn_x4
RELU = mybir.ActivationFunctionType.Relu

G, S, M, H, E, C = 8, 1024, 512, 512, 8, 64
FLOPS = 2 * G * (E * C) * M * S + 2 * E * (G * C) * M * H

P = 128
PACK = 4
K_PASS = P * PACK
WIDTH = 512
PASSES = S // K_PASS
BANKS_PER_GROUP = (E * C) // P
EXPERTS_PER_BANK = P // C
HALVES = 2
GROUPS_PER_HALF = G // HALVES
TILES_PER_HALF = (GROUPS_PER_HALF * C) // P

RUN = 4
VECTOR_COLUMNS = 344
RESULT_BUFS = 8
SHARE_EVERY = 100
SHARE_PHASE = 0
HEAD_PIECES = 2
EARLY_VECTOR_COLUMNS = 256
EARLY_STEPS = 6
TENSOR_COLUMNS = 256
REGROUPED_BANKS = 2
PRODUCT_BANKS = 6
RAW_BUFS = 22
GROUPED_BUFS = 4
EVACUATE_LAG = 2
EARLY_EXPERTS = 0
FIRST_WI_AFTER = 4
WI_STRIDE = 1
LEAD = 2
SHARED_KIND = "x"
SHARED_K = 1
WI_COLUMNS = 352
LATE_COLUMNS = 512
FIRST_LATE_COLUMNS = 512
FIRST_LATE = 2
FIRST_SHARED = 0
FINAL_PIECES = 2


def tile_flaxpositionwisemoelayer_pa_t_kernel(tc, dispatch_mask, x, wi, out):
    nc = tc.nc

    mask_slabs = dispatch_mask.rearrange("g (k p j) e c -> g k p j (e c)", p=P, j=PACK)
    x_slabs = x.rearrange("g (k p j) m -> g k p j m", p=P, j=PACK)
    wi_slabs = wi.rearrange("e (j p) h -> e p j h", p=P)
    out_halves = out.rearrange(
        "e (a g) (q b) h -> e a (g q) b h", a=HALVES, b=TILES_PER_HALF
    )

    stream = []
    for g in range(G):
        for k in range(PASSES):
            stream.append(("mask", g, k))
            stream.append(("x", g, k))
        stream += [("wi", e, 0) for e in range(EARLY_EXPERTS) if FIRST_WI_AFTER + e * WI_STRIDE == g]
    stream_length = len(stream)
    stream += [("wi", e, 0) for e in range(EARLY_EXPERTS, E)]

    def is_shared(n):
        kind, i, k = stream[n]
        return kind == SHARED_KIND and k < SHARED_K and i >= FIRST_SHARED

    with ExitStack() as ctx:
        raw_pool = ctx.enter_context(tc.tile_pool(name="raw", bufs=RAW_BUFS))
        grouped_pool = ctx.enter_context(tc.tile_pool(name="grouped", bufs=GROUPED_BUFS))
        operand_pool = ctx.enter_context(tc.tile_pool(name="operands", bufs=3))
        keep_pool = ctx.enter_context(tc.tile_pool(name="keep", bufs=1))
        result_pool = ctx.enter_context(tc.tile_pool(name="result", bufs=RESULT_BUFS))
        psum = ctx.enter_context(tc.psum_pool(name="psum", bufs=8))
        ctx.enter_context(tc.manual_schedule())

        identity = keep_pool.tile([P, P], BF16)
        make_identity(nc, identity[:])
        wi_codes = keep_pool.tile([P, E, H], U32, align_bytes=64)
        wi_scales = keep_pool.tile([P, E, H], U8, align_bytes=64)

        raws = {}

        def fetch(n):
            if n < len(stream):
                kind, i, k = stream[n]
                if kind == "mask":
                    source = mask_slabs[i, k]
                elif kind == "x":
                    source = x_slabs[i, k]
                else:
                    source = wi_slabs[i]
                raw = raw_pool.tile([P, PACK, WIDTH], BF16)
                pieces = HEAD_PIECES if n == 0 else 1
                for w in range(pieces):
                    columns = slice(w * WIDTH // pieces, (w + 1) * WIDTH // pieces)
                    nc.sync.dma_start(out=raw[:, :, columns], in_=source[:, :, columns])
                raws[n] = raw

        def regroup_on_tensor(raw):
            bank = psum.tile([P, TENSOR_COLUMNS, PACK], BF16, tag="regrouped", bufs=REGROUPED_BANKS)
            for w in range(0, TENSOR_COLUMNS, P):
                first = WIDTH - TENSOR_COLUMNS + w
                nc.tensor.matmul(
                    out=bank[:, w : w + P, :].rearrange("p w j -> p j w"),
                    lhsT=identity[:],
                    rhs=raw[:, :, first : first + P],
                    start=True,
                    stop=True,
                )
            return bank

        def regroup(raw, vector_columns, bank):
            grouped = grouped_pool.tile([P, WIDTH, PACK], BF16, align_bytes=64)
            nc.vector.tensor_copy(
                out=grouped[:, :vector_columns, :].rearrange("p (w i) j -> p w j i", i=RUN),
                in_=raw[:, :, :vector_columns].rearrange("p j (w i) -> p w j i", i=RUN),
            )
            if bank is not None:
                nc.scalar.copy(
                    out=grouped[:, vector_columns:, :].rearrange("p w j -> p (w j)"),
                    in_=bank[:].rearrange("p w j -> p (w j)"),
                )
            elif vector_columns < WIDTH:
                nc.scalar.copy(
                    out=grouped[:, vector_columns:, :].rearrange("p (w i) j -> p w j i", i=RUN),
                    in_=raw[:, :, vector_columns:].rearrange("p j (w i) -> p w j i", i=RUN),
                )
            return grouped

        def quantise(values, codes, scales):
            nc.vector.quantize_mx(out=codes.bitcast(FP8X4), scales=scales, in_=values)

        operands = {}

        def quantise_slab(n, grouped):
            kind, i, k = stream[n]
            values = grouped[:].rearrange("p w j -> p (w j)")
            if kind == "wi":
                quantise(values, wi_codes[:, i, :], wi_scales[:, i, :])
                return
            if i not in operands:
                mask_codes = operand_pool.tile([P, PASSES, WIDTH], U32, align_bytes=64)
                mask_scales = operand_pool.tile([P, PASSES, WIDTH], U8, align_bytes=64)
                x_codes = operand_pool.tile([P, PASSES, WIDTH], U32, align_bytes=64)
                x_scales = operand_pool.tile([P, PASSES, WIDTH], U8, align_bytes=64)
                operands[i] = {"mask": (mask_codes, mask_scales), "x": (x_codes, x_scales)}
            codes, scales = operands[i][kind]
            quantise(values, codes[:, k, :], scales[:, k, :])

        dispatched = {}
        for n in range(BANKS_PER_GROUP):
            for a in range(HALVES):
                dispatched[n, a] = keep_pool.tile(
                    [P, EXPERTS_PER_BANK, TILES_PER_HALF, GROUPS_PER_HALF, C // TILES_PER_HALF, PACK],
                    BF16,
                    name="dispatched%d%d" % (n, a),
                    align_bytes=64,
                )

        def dispatch(g, n):
            mask_codes, mask_scales = operands[g]["mask"]
            x_codes, x_scales = operands[g]["x"]
            bank = psum.tile([P, PACK, P], F32, tag="bank", bufs=PRODUCT_BANKS)
            columns = slice(n * P, (n + 1) * P)
            for j in range(PACK):
                m_tile = slice(j * P, (j + 1) * P)
                for k in range(PASSES):
                    nc.tensor.matmul_mx(
                        out=bank[:, j, :],
                        lhsT=x_codes[:, k, m_tile].bitcast(FP8X4),
                        lhsT_scale=x_scales[:, k, m_tile],
                        rhs=mask_codes[:, k, columns].bitcast(FP8X4),
                        rhs_scale=mask_scales[:, k, columns],
                        start=(k == 0),
                        stop=(k == PASSES - 1),
                    )
            return bank

        def evacuate(bank, g, n):
            a, g_in_half = divmod(g, GROUPS_PER_HALF)
            nc.scalar.copy(
                out=dispatched[n, a][:, :, :, g_in_half, :, :],
                in_=bank[:].rearrange(
                    "p j (e q b) -> p e b q j", e=EXPERTS_PER_BANK, b=TILES_PER_HALF
                ),
            )

        def project(e, a):
            n, member = divmod(e, EXPERTS_PER_BANK)
            d_codes = operand_pool.tile([P, TILES_PER_HALF * P], U32, align_bytes=64)
            d_scales = operand_pool.tile([P, TILES_PER_HALF * P], U8, align_bytes=64)
            quantise(
                dispatched[n, a][:, member].rearrange("p b g q j -> p (b g q j)"),
                d_codes[:],
                d_scales[:],
            )
            accs = []
            for b in range(TILES_PER_HALF):
                rows = slice(b * P, (b + 1) * P)
                acc = psum.tile([P, H], F32, tag="bank", bufs=PRODUCT_BANKS)
                nc.tensor.matmul_mx(
                    out=acc[:],
                    lhsT=d_codes[:, rows].bitcast(FP8X4),
                    lhsT_scale=d_scales[:, rows],
                    rhs=wi_codes[:, e, :].bitcast(FP8X4),
                    rhs_scale=wi_scales[:, e, :],
                    start=True,
                    stop=True,
                )
                accs.append(acc)
            return accs

        def store(accs, e, a, share):
            result = result_pool.tile([P, TILES_PER_HALF, H], F32)
            if (e, a) == (E - 1, HALVES - 1):
                for h in range(0, H, H // FINAL_PIECES):
                    columns = slice(h, h + H // FINAL_PIECES)
                    nc.scalar.activation(out=result[:, 0, columns], in_=accs[0][:, columns], func=RELU)
                    nc.vector.tensor_scalar_max(result[:, 1, columns], accs[1][:, columns], 0.0)
                    for b in range(TILES_PER_HALF):
                        nc.sync.dma_start(out=out_halves[e, a][:, b, columns], in_=result[:, b, columns])
                return
            nc.scalar.activation(out=result[:, 0, :], in_=accs[0][:], func=RELU)
            last = (e, a) == (E - 1, HALVES - 1)
            if last:
                nc.sync.dma_start(out=out_halves[e, a][:, 0, :], in_=result[:, 0, :])
            if share:
                nc.vector.tensor_scalar_max(result[:, 1, :], accs[1][:], 0.0)
            else:
                nc.scalar.activation(out=result[:, 1, :], in_=accs[1][:], func=RELU)
            if last:
                nc.sync.dma_start(out=out_halves[e, a][:, 1, :], in_=result[:, 1, :])
            else:
                nc.sync.dma_start(out=out_halves[e, a], in_=result[:])

        for n in range(RAW_BUFS - 1):
            fetch(n)
        grouped_slabs = {}
        regrouped_banks = {}
        to_dispatch = []
        full_banks = []
        to_project = []
        to_store = []
        step = 0
        while step <= stream_length or to_dispatch or full_banks:
            fetch(step + RAW_BUFS - 1)
            if step + LEAD < stream_length and is_shared(step + LEAD):
                regrouped_banks[step + LEAD] = regroup_on_tensor(raws[step + LEAD])
            if step < stream_length:
                if is_shared(step):
                    columns = WIDTH - TENSOR_COLUMNS
                elif step < EARLY_STEPS:
                    columns = EARLY_VECTOR_COLUMNS
                elif stream[step][0] == "wi":
                    columns = WI_COLUMNS
                else:
                    columns = VECTOR_COLUMNS
                grouped_slabs[step] = regroup(raws[step], columns, regrouped_banks.get(step))
            storing = to_store
            to_store = [(project(e, a), e, a) for e, a in to_project]
            to_project = []
            ready = step - 1
            if 0 <= ready < stream_length:
                kind, i, k = stream[ready]
                quantise_slab(ready, grouped_slabs[ready])
                if kind == "wi":
                    to_project.append((i, 0))
                elif (kind, k) == ("x", PASSES - 1):
                    to_dispatch += [(i, n) for n in range(BANKS_PER_GROUP)]
            if full_banks and full_banks[0][0] + EVACUATE_LAG <= step:
                filled, bank, g, n = full_banks.pop(0)
                evacuate(bank, g, n)
            if to_dispatch:
                g, n = to_dispatch.pop(0)
                full_banks.append((step, dispatch(g, n), g, n))
            for accs, e, a in storing:
                store(accs, e, a, False)
            step += 1

        halves = [(e, 1) for e in range(EARLY_EXPERTS)]
        halves += [(e, a) for e in range(EARLY_EXPERTS, E) for a in range(HALVES)]
        halves = to_project + halves
        late = stream_length
        if EARLY_EXPERTS == 0:
            grouped_first = regroup(raws[late], FIRST_LATE_COLUMNS, None)
            quantise_slab(late, grouped_first)
            late += 1
        grouped_late = {}
        for i, (e, a) in enumerate(halves):
            storing = to_store
            to_store = [(project(e, a), e, a)]
            for n in list(grouped_late):
                quantise_slab(n, grouped_late.pop(n))
            if i % 2 == 0 and late < len(stream):
                grouped_late[late] = regroup(raws[late], FIRST_LATE_COLUMNS if late < stream_length + FIRST_LATE else LATE_COLUMNS, None)
                late += 1
            for accs, e2, a2 in storing:
                store(accs, e2, a2, i % SHARE_EVERY == SHARE_PHASE)
        for accs, e2, a2 in to_store:
            store(accs, e2, a2, True)
